import numpy as np
import ml_dtypes


def mxq(x, axis, fmt="e4m3"):
    dtype, down = {"e4m3": (ml_dtypes.float8_e4m3fn, 7), "e5m2": (ml_dtypes.float8_e5m2, 14)}[fmt]
    v = np.moveaxis(np.asarray(x, np.float32).astype(ml_dtypes.bfloat16).astype(np.float64), axis, -1)
    blocks = v.reshape(v.shape[:-1] + (-1, 32))
    amax = np.abs(blocks).max(-1, keepdims=True)
    byte = np.maximum(np.where(amax > 0, np.frexp(amax)[1] - 1 + 127, 0) - down, 1)
    scale = np.exp2(byte - 127.0)
    codes = (blocks / scale).astype(np.float32).astype(dtype).astype(np.float64)
    return np.moveaxis((codes * scale).reshape(v.shape), -1, axis)


WIDE = False


def mx_kscale(k):
    if not WIDE:
        return np.ones(k)
    levels = np.array([10, -10, 5, -5, 0])
    if k % 512:
        return np.exp2(np.random.permutation(np.resize(levels, k // 32))).repeat(32)
    a = np.empty((k // 512, 16))
    for p in range(k // 512):
        a[p, :8] = np.random.permutation(np.resize(levels, 8))
        for g in range(8):
            far = levels[np.abs(levels - a[p, g]) >= 10]
            a[p, g + 8] = far[np.random.randint(len(far))]
    return np.exp2(a.ravel()).repeat(32)


BF16 = ml_dtypes.bfloat16


def bf(x):
    return np.asarray(x, np.float32).astype(BF16)


def f64(x):
    return np.asarray(x).astype(np.float64)


B, HH, WW, C, NH, KD, WS, SS = 2, 64, 64, 512, 2, 64, 8, 4
GH, GW, T, F = HH // WS, WW // WS, WS * WS, NH * KD
N = B * GH * GW


def setup_inputs():
    s = mx_kscale(C)

    def weight():
        return bf(np.random.standard_normal((C, NH, KD)) / np.sqrt(C) / s[:, None, None])

    def bias():
        return bf(np.random.standard_normal((NH, KD)) * 0.3)

    return {"x": bf(np.random.standard_normal((B, HH, WW, C)) * s), "wq": weight(), "bq": bias(),
            "wk": weight(), "bk": bias(), "wv": weight(), "bv": bias()}


def reference(x, wq, bq, wk, bk, wv, bv):
    shifted = np.roll(f64(x), shift=(-SS, -SS), axis=(1, 2))
    win = shifted.reshape(B, GH, WS, GW, WS, C).swapaxes(2, 3).reshape(N * T, C)
    wn = mxq(win, 1, "e4m3")
    q = (wn @ mxq(f64(wq).reshape(C, F), 0, "e4m3")).reshape(N, T, NH, KD) + f64(bq)
    k = (wn @ mxq(f64(wk).reshape(C, F), 0, "e4m3")).reshape(N, T, NH, KD) + f64(bk)
    v = (wn @ mxq(f64(wv).reshape(C, F), 0, "e4m3")).reshape(N, T, NH, KD) + f64(bv)
    return q, k, v

@@ -1,0 +1,220 @@
+from contextlib import ExitStack
+
+import concourse.mybir as mybir
+from concourse.masks import make_identity
+
+FP8X4 = mybir.dt.float8_e4m3fn_x4
+BF16 = mybir.dt.bfloat16
+F32 = mybir.dt.float32
+U32 = mybir.dt.uint32
+U8 = mybir.dt.uint8
+
+P = 128
+FLOPS = 2 * 8192 * 512 * 384
+MANUAL = True
+LOOK_T = 3
+LOOK_Q = 2
+SLABS = (0, 1, 3, 2, 7, 4, 5, 6)
+
+
+def tile_windowattentionblock_pa_t_kernel(tc, x, wq, bq, wk, bk, wv, bv, out_0, out_1, out_2):
+    nc = tc.nc
+    weights = (wq, wk, wv)
+    biases = (bq, bk, bv)
+    outs = [o.rearrange("n (ti tj) h d -> (n ti) (tj h d)", tj=8) for o in (out_0, out_1, out_2)]
+    xc = x.rearrange("b i (aj rj) c -> (b i aj) (rj c)", rj=8)
+
+    with ExitStack() as ctx:
+        const = ctx.enter_context(tc.tile_pool(name="const", bufs=1))
+        xpool = ctx.enter_context(tc.tile_pool(name="xpool", bufs=1))
+        gpool = ctx.enter_context(tc.tile_pool(name="gpool", bufs=3))
+        qpool = ctx.enter_context(tc.tile_pool(name="qpool", bufs=4))
+        opool = ctx.enter_context(tc.tile_pool(name="opool", bufs=8))
+        psum_t = ctx.enter_context(tc.psum_pool(name="psum_t", bufs=2))
+        psum_o = ctx.enter_context(tc.psum_pool(name="psum_o", bufs=6))
+        if MANUAL:
+            ctx.enter_context(tc.manual_schedule())
+
+        b_row = const.tile([P, 512], BF16, name="b_row")
+        nc.vector.memset(b_row[:], 0.0)
+        ones = const.tile([P, P], BF16, name="ones")
+        nc.vector.memset(ones[:], 1.0)
+
+        w_raw = const.tile([P, 3, 4, P], BF16, name="w_raw")
+        for m in range(3):
+            nc.scalar.dma_start(
+                out=w_raw[:, m, :, :].rearrange("p (u e) f -> p u (e f)", u=2),
+                in_=weights[m].rearrange("(p u e) h d -> p u (e h d)", u=2, e=2),
+            )
+        x_sb = {}
+        for pos, k in enumerate(SLABS):
+            x_t = xpool.tile([P, 4096], BF16, name="x%d" % k)
+            x_sb[k] = x_t
+            b, a = divmod(k, 4)
+            c0 = (b * 64 + 16 * a + 4) * 8
+            if pos == 0:
+                nc.sync.dma_start(out=x_t[:, 2048:4096], in_=xc[c0:c0 + P, 2048:4096])
+                nc.sync.dma_start(out=x_t[:, 0:2048], in_=xc[c0:c0 + P, 0:2048])
+                for m in range(3):
+                    nc.sync.dma_start(
+                        out=b_row[0:1, m * P:(m + 1) * P],
+                        in_=biases[m].rearrange("(o h) d -> o (h d)", o=1),
+                    )
+            elif a < 3:
+                nc.sync.dma_start(out=x_t[:], in_=xc[c0:c0 + P, :])
+            else:
+                for s in range(4):
+                    cs = c0 + 32 * s if s < 3 else b * 512
+                    nc.sync.dma_start(out=x_t[s:P:4, :], in_=xc[cs:cs + 32, :])
+
+
+        ident = const.tile([P, P], F32, name="ident")
+        make_identity(nc, ident[:])
+        pa = const.tile([P, P], F32, name="pa")
+        pb = const.tile([P, P], F32, name="pb")
+        src = ident[:].rearrange("p (g t a) -> p g a t", g=2, t=8)
+        pav = pa[:].rearrange("p (g a t) -> p g a t", g=2, a=8)
+        pbv = pb[:].rearrange("p (g a t) -> p g a t", g=2, a=8)
+        nc.gpsimd.tensor_copy(out=pav, in_=src)
+        nc.gpsimd.tensor_copy(out=pbv[:, :, 0:7, :], in_=src[:, :, 1:8, :])
+        nc.gpsimd.tensor_copy(out=pbv[:, :, 7:8, :], in_=src[:, :, 0:1, :])
+        paw = const.tile([P, P], F32, name="paw")
+        pbw = const.tile([P, P], F32, name="pbw")
+        srcw = ident[:].rearrange("p (tl a g th) -> p g a th tl", tl=4, a=8, g=2)
+        pawv = paw[:].rearrange("p (g a th tl) -> p g a th tl", g=2, a=8, th=2)
+        pbwv = pbw[:].rearrange("p (g a th tl) -> p g a th tl", g=2, a=8, th=2)
+        for gg in range(2):
+            nc.vector.tensor_copy(out=pawv[:, gg, :, :, :], in_=srcw[:, gg, :, :, :])
+            nc.vector.tensor_copy(out=pbwv[:, gg, 0:7, :, :], in_=srcw[:, gg, 1:8, :, :])
+            nc.vector.tensor_copy(out=pbwv[:, gg, 7:8, :, :], in_=srcw[:, gg, 0:1, :, :])
+
+        w_grp = const.tile([P, 3, P, 4], BF16, name="w_grp", align_bytes=64)
+        w_codes = const.tile([P, 384], U32, name="w_codes", align_bytes=64)
+        w_scales = const.tile([P, 384], U8, name="w_scales", align_bytes=64)
+        for m in range(3):
+            nc.vector.tensor_copy(out=w_grp[:, m, :, :], in_=w_raw[:, m, :, :].rearrange("p t f -> p f t"))
+        nc.vector.quantize_mx(
+            out=w_codes[:, 0:256].bitcast(FP8X4),
+            scales=w_scales[:, 0:256],
+            in_=w_grp[:, 0:2, :, :].rearrange("p m f t -> p (m f t)"),
+        )
+        nc.vector.quantize_mx(
+            out=w_codes[:, 256:384].bitcast(FP8X4),
+            scales=w_scales[:, 256:384],
+            in_=w_grp[:, 2, :, :].rearrange("p f t -> p (f t)"),
+        )
+
+        bias_sb = const.tile([P, 3, P], F32, name="bias_sb")
+
+        def spread_bias():
+            bias_ps = psum_o.tile([P, 512], F32, name="acc")
+            nc.tensor.matmul(out=bias_ps[:], lhsT=ones[:], rhs=b_row[:], start=True, stop=True)
+            nc.scalar.copy(out=bias_sb[:].rearrange("p m f -> p (m f)"), in_=bias_ps[:, 0:384])
+
+        units = [(k, hb) for k in SLABS for hb in range(2)]
+        state = {}
+
+        def transposes(h):
+            ti, hb = units[h]
+            if ti % 4 == 3:
+                perm = paw if hb == 0 else pbw
+            else:
+                perm = pa if hb == 0 else pb
+            xf = x_sb[ti][:].bitcast(F32)
+            g = gpool.tile([P, 2048], BF16, name="g", align_bytes=64)
+            gf = g[:].bitcast(F32).rearrange("p (a r u) -> p a r u", a=4, u=2)
+            for a2 in range(2):
+                xt = psum_t.tile([P, 2, 2, P], F32, name="xt")
+                for a in range(2):
+                    rj = (4 * hb + 2 * a2 + a + 4) % 8
+                    for u in range(2):
+                        c0 = rj * 256
+                        nc.tensor.transpose(xt[:, a, u, :], xf[:, c0 + u:c0 + 256:2], perm[:])
+                nc.scalar.copy(out=gf[:, 2 * a2:2 * a2 + 2, :, :], in_=xt[:].rearrange("p a u r -> p a r u"))
+            state[("g", h)] = g
+
+        def quantise(h):
+            g = state[("g", h)]
+            codes = qpool.tile([P, 512], U32, name="codes", align_bytes=64)
+            scales = qpool.tile([P, 512], U8, name="scales", align_bytes=64)
+            nc.vector.quantize_mx(out=codes[:].bitcast(FP8X4), scales=scales[:], in_=g[:])
+            state[("q", h)] = (codes, scales)
+
+        def mx(out, codes, scales, a, n0, n1):
+            cols = slice(a * P, (a + 1) * P)
+            nc.tensor.matmul_mx(
+                out=out,
+                lhsT=codes[:, cols].bitcast(FP8X4),
+                lhsT_scale=scales[:, cols],
+                rhs=w_codes[:, n0:n1].bitcast(FP8X4),
+                rhs_scale=w_scales[:, n0:n1],
+                start=True,
+                stop=True,
+            )
+
+        def project(h, half):
+            ti, hb = units[h]
+            codes, scales = state[("q", h)]
+            if hb == 0 and half == 0:
+                state[("o", ti)] = opool.tile([P, 3, 8, P], F32, name="o_sb")
+            o_sb = state[("o", ti)]
+            if half == 0:
+                state[("z", h)] = psum_o.tile([P, 4, P], F32, name="acc")
+            zb = state[("z", h)]
+            qk = psum_o.tile([P, 2, 2, P], F32, name="acc")
+            for i in range(2):
+                a = 2 * half + i
+                mx(qk[:, i, :, :].rearrange("p m f -> p (m f)"), codes, scales, a, 0, 256)
+                mx(zb[:, a, :], codes, scales, a, 256, 384)
+            t0 = 4 * hb + 2 * half
+            nc.vector.tensor_tensor(
+                out=o_sb[:, 0:2, t0:t0 + 2, :],
+                in0=qk[:].rearrange("p t m f -> p m t f"),
+                in1=bias_sb[:, 0:2, :].unsqueeze(2).to_broadcast([P, 2, 2, P]),
+                op=mybir.AluOpType.add,
+            )
+            if half == 1:
+                v_sb = o_sb[:, 2, 4 * hb:4 * hb + 4, :]
+                nc.scalar.copy(out=v_sb, in_=zb[:])
+                nc.gpsimd.tensor_tensor(
+                    out=v_sb,
+                    in0=v_sb,
+                    in1=bias_sb[:, 2:3, :].to_broadcast([P, 4, P]),
+                    op=mybir.AluOpType.add,
+                )
+
+        def store(ti, t0, t1):
+            o_sb = state[("o", ti)]
+            for m in range(3):
+                nc.sync.dma_start(
+                    out=outs[m][ti * P:(ti + 1) * P, t0 * P:t1 * P],
+                    in_=o_sb[:, m, t0:t1, :].rearrange("p t f -> p (t f)"),
+                )
+
+        n_units = len(units)
+        done = {"t": 0, "q": 0}
+
+        def transposes_upto(last):
+            while done["t"] <= min(last, n_units - 1):
+                transposes(done["t"])
+                done["t"] += 1
+
+        def quantise_upto(last):
+            while done["q"] <= min(last, n_units - 1):
+                quantise(done["q"])
+                done["q"] += 1
+
+        transposes_upto(0)
+        quantise_upto(0)
+        for h in range(n_units):
+            ti, hb = units[h]
+            transposes_upto(h + min(LOOK_T, h + 1))
+            if h == 0:
+                spread_bias()
+            project(h, 0)
+            quantise_upto(h + min(LOOK_Q, h + 1))
+            project(h, 1)
+            if h >= n_units - 2:
+                store(ti, 4 * hb, 4 * hb + 4)
+            elif hb == 1:
+                store(ti, 0, 8)

@@ -12,9 +12,9 @@ U8 = mybir.dt.uint8
 P = 128
 FLOPS = 2 * 8192 * 512 * 384
 MANUAL = True
-LOOK_T = 3
-LOOK_Q = 2
-SLABS = (0, 1, 3, 2, 7, 4, 5, 6)
+LOOK_T = 1
+LOOK_Q = 1
+SLABS = (0, 1, 2, 4, 3, 7, 5, 6)
 
 
 def tile_windowattentionblock_pa_t_kernel(tc, x, wq, bq, wk, bk, wv, bv, out_0, out_1, out_2):
@@ -41,31 +41,42 @@ def tile_windowattentionblock_pa_t_kernel(tc, x, wq, bq, wk, bk, wv, bv, out_0, 
         nc.vector.memset(ones[:], 1.0)
 
         w_raw = const.tile([P, 3, 4, P], BF16, name="w_raw")
+        x_sb = {}
+
+        def load_slabs(first, n):
+            x_t = xpool.tile([P, n, 4096], BF16, name="x%d" % first)
+            b, a = divmod(first, 4)
+            c0 = (b * 64 + 16 * a + 4) * 8
+            nc.sync.dma_start(out=x_t[:], in_=xc[c0:c0 + n * P, :].rearrange("(s p) f -> p s f", p=P))
+            for i in range(n):
+                x_sb[first + i] = x_t[:, i, :]
+
+        x0 = xpool.tile([P, 4096], BF16, name="x0")
+        x_sb[0] = x0[:]
+        nc.sync.dma_start(out=x0[:, 2048:3072], in_=xc[32:32 + P, 2048:3072])
+        nc.sync.dma_start(out=x0[:, 3072:4096], in_=xc[32:32 + P, 3072:4096])
         for m in range(3):
-            nc.scalar.dma_start(
+            nc.sync.dma_start(
                 out=w_raw[:, m, :, :].rearrange("p (u e) f -> p u (e f)", u=2),
                 in_=weights[m].rearrange("(p u e) h d -> p u (e h d)", u=2, e=2),
             )
-        x_sb = {}
-        for pos, k in enumerate(SLABS):
-            x_t = xpool.tile([P, 4096], BF16, name="x%d" % k)
-            x_sb[k] = x_t
-            b, a = divmod(k, 4)
-            c0 = (b * 64 + 16 * a + 4) * 8
-            if pos == 0:
-                nc.sync.dma_start(out=x_t[:, 2048:4096], in_=xc[c0:c0 + P, 2048:4096])
-                nc.sync.dma_start(out=x_t[:, 0:2048], in_=xc[c0:c0 + P, 0:2048])
-                for m in range(3):
-                    nc.sync.dma_start(
-                        out=b_row[0:1, m * P:(m + 1) * P],
-                        in_=biases[m].rearrange("(o h) d -> o (h d)", o=1),
-                    )
-            elif a < 3:
-                nc.sync.dma_start(out=x_t[:], in_=xc[c0:c0 + P, :])
-            else:
-                for s in range(4):
-                    cs = c0 + 32 * s if s < 3 else b * 512
-                    nc.sync.dma_start(out=x_t[s:P:4, :], in_=xc[cs:cs + 32, :])
+        nc.sync.dma_start(out=x0[:, 0:2048], in_=xc[32:32 + P, 0:2048])
+        load_slabs(1, 1)
+        for m in range(3):
+            nc.scalar.dma_start(
+                out=b_row[0:1, m * P:(m + 1) * P],
+                in_=biases[m].rearrange("(o h) d -> o (h d)", o=1),
+            )
+        load_slabs(2, 1)
+        load_slabs(4, 1)
+        xwrap = xpool.tile([P, 2, 4096], BF16, name="xwrap")
+        xcb = xc.rearrange("(b c) f -> c b f", b=2)
+        nc.sync.dma_start(out=xwrap[0:P:2, :, :], in_=xcb[416:480, :, :])
+        nc.sync.dma_start(out=xwrap[1:P:4, :, :], in_=xcb[480:512, :, :])
+        nc.sync.dma_start(out=xwrap[3:P:4, :, :], in_=xcb[0:32, :, :])
+        x_sb[3] = xwrap[:, 0, :]
+        x_sb[7] = xwrap[:, 1, :]
+        load_slabs(5, 2)
 
 
         ident = const.tile([P, P], F32, name="ident")
@@ -80,13 +91,16 @@ def tile_windowattentionblock_pa_t_kernel(tc, x, wq, bq, wk, bk, wv, bv, out_0, 
         nc.gpsimd.tensor_copy(out=pbv[:, :, 7:8, :], in_=src[:, :, 0:1, :])
         paw = const.tile([P, P], F32, name="paw")
         pbw = const.tile([P, P], F32, name="pbw")
-        srcw = ident[:].rearrange("p (tl a g th) -> p g a th tl", tl=4, a=8, g=2)
-        pawv = paw[:].rearrange("p (g a th tl) -> p g a th tl", g=2, a=8, th=2)
-        pbwv = pbw[:].rearrange("p (g a th tl) -> p g a th tl", g=2, a=8, th=2)
-        for gg in range(2):
-            nc.vector.tensor_copy(out=pawv[:, gg, :, :, :], in_=srcw[:, gg, :, :, :])
-            nc.vector.tensor_copy(out=pbwv[:, gg, 0:7, :, :], in_=srcw[:, gg, 1:8, :, :])
-            nc.vector.tensor_copy(out=pbwv[:, gg, 7:8, :, :], in_=srcw[:, gg, 0:1, :, :])
+        src0 = ident[:, 0:P:2].rearrange("p (t a) -> p a t", t=8)
+        src1 = ident[:].rearrange("p (tl a r) -> p r a tl", tl=4, a=8)
+        for dst, shift in ((paw, 0), (pbw, 1)):
+            d0 = dst[:, 0:64].rearrange("p (a t) -> p a t", a=8)
+            d1 = dst[:, 64:P].rearrange("p (a th tl) -> p th a tl", a=8, th=2)
+            nc.vector.tensor_copy(out=d0[:, 0:8 - shift, :], in_=src0[:, shift:8, :])
+            nc.vector.tensor_copy(out=d1[:, :, 0:8 - shift, :], in_=src1[:, 1:4:2, shift:8, :])
+            if shift:
+                nc.vector.tensor_copy(out=d0[:, 7:8, :], in_=src0[:, 0:1, :])
+                nc.vector.tensor_copy(out=d1[:, :, 7:8, :], in_=src1[:, 1:4:2, 0:1, :])
 
         w_grp = const.tile([P, 3, P, 4], BF16, name="w_grp", align_bytes=64)
         w_codes = const.tile([P, 384], U32, name="w_codes", align_bytes=64)
@@ -120,7 +134,7 @@ def tile_windowattentionblock_pa_t_kernel(tc, x, wq, bq, wk, bk, wv, bv, out_0, 
                 perm = paw if hb == 0 else pbw
             else:
                 perm = pa if hb == 0 else pb
-            xf = x_sb[ti][:].bitcast(F32)
+            xf = x_sb[ti].bitcast(F32)
             g = gpool.tile([P, 2048], BF16, name="g", align_bytes=64)
             gf = g[:].bitcast(F32).rearrange("p (a r u) -> p a r u", a=4, u=2)
             for a2 in range(2):

@@ -53,17 +53,16 @@ def tile_windowattentionblock_pa_t_kernel(tc, x, wq, bq, wk, bk, wv, bv, out_0, 
 
         x0 = xpool.tile([P, 4096], BF16, name="x0")
         x_sb[0] = x0[:]
-        nc.sync.dma_start(out=x0[:, 2048:3072], in_=xc[32:32 + P, 2048:3072])
-        nc.sync.dma_start(out=x0[:, 3072:4096], in_=xc[32:32 + P, 3072:4096])
+        nc.sync.dma_start(out=x0[:, 2048:4096], in_=xc[32:32 + P, 2048:4096])
+        nc.sync.dma_start(out=x0[:, 0:2048], in_=xc[32:32 + P, 0:2048])
         for m in range(3):
             nc.sync.dma_start(
                 out=w_raw[:, m, :, :].rearrange("p (u e) f -> p u (e f)", u=2),
                 in_=weights[m].rearrange("(p u e) h d -> p u (e h d)", u=2, e=2),
             )
-        nc.sync.dma_start(out=x0[:, 0:2048], in_=xc[32:32 + P, 0:2048])
         load_slabs(1, 1)
         for m in range(3):
-            nc.scalar.dma_start(
+            nc.sync.dma_start(
                 out=b_row[0:1, m * P:(m + 1) * P],
                 in_=biases[m].rearrange("(o h) d -> o (h d)", o=1),
             )
@@ -166,12 +165,9 @@ def tile_windowattentionblock_pa_t_kernel(tc, x, wq, bq, wk, bk, wv, bv, out_0, 
                 stop=True,
             )
 
-        def project(h, half):
+        def passes(h, half):
             ti, hb = units[h]
             codes, scales = state[("q", h)]
-            if hb == 0 and half == 0:
-                state[("o", ti)] = opool.tile([P, 3, 8, P], F32, name="o_sb")
-            o_sb = state[("o", ti)]
             if half == 0:
                 state[("z", h)] = psum_o.tile([P, 4, P], F32, name="acc")
             zb = state[("z", h)]
@@ -180,6 +176,15 @@ def tile_windowattentionblock_pa_t_kernel(tc, x, wq, bq, wk, bk, wv, bv, out_0, 
                 a = 2 * half + i
                 mx(qk[:, i, :, :].rearrange("p m f -> p (m f)"), codes, scales, a, 0, 256)
                 mx(zb[:, a, :], codes, scales, a, 256, 384)
+            state[("qk", h, half)] = qk
+
+        def finish(h, half):
+            ti, hb = units[h]
+            if hb == 0 and half == 0:
+                state[("o", ti)] = opool.tile([P, 3, 8, P], F32, name="o_sb")
+            o_sb = state[("o", ti)]
+            zb = state[("z", h)]
+            qk = state[("qk", h, half)]
             t0 = 4 * hb + 2 * half
             nc.vector.tensor_tensor(
                 out=o_sb[:, 0:2, t0:t0 + 2, :],
@@ -223,11 +228,13 @@ def tile_windowattentionblock_pa_t_kernel(tc, x, wq, bq, wk, bk, wv, bv, out_0, 
         for h in range(n_units):
             ti, hb = units[h]
             transposes_upto(h + min(LOOK_T, h + 1))
+            passes(h, 0)
+            passes(h, 1)
             if h == 0:
                 spread_bias()
-            project(h, 0)
             quantise_upto(h + min(LOOK_Q, h + 1))
-            project(h, 1)
+            finish(h, 0)
+            finish(h, 1)
             if h >= n_units - 2:
                 store(ti, 4 * hb, 4 * hb + 4)
             elif hb == 1:

@@ -235,7 +235,7 @@ def tile_windowattentionblock_pa_t_kernel(tc, x, wq, bq, wk, bk, wv, bv, out_0, 
             quantise_upto(h + min(LOOK_Q, h + 1))
             finish(h, 0)
             finish(h, 1)
-            if h >= n_units - 2:
+            if h >= n_units - 6:
                 store(ti, 4 * hb, 4 * hb + 4)
             elif hb == 1:
                 store(ti, 0, 8)

@@ -150,7 +150,13 @@ def tile_windowattentionblock_pa_t_kernel(tc, x, wq, bq, wk, bk, wv, bv, out_0, 
             g = state[("g", h)]
             codes = qpool.tile([P, 512], U32, name="codes", align_bytes=64)
             scales = qpool.tile([P, 512], U8, name="scales", align_bytes=64)
-            nc.vector.quantize_mx(out=codes[:].bitcast(FP8X4), scales=scales[:], in_=g[:])
+            for half in range(2):
+                cols = slice(half * 256, half * 256 + 256)
+                nc.vector.quantize_mx(
+                    out=codes[:, cols].bitcast(FP8X4),
+                    scales=scales[:, cols],
+                    in_=g[:, half * 1024:half * 1024 + 1024],
+                )
             state[("q", h)] = (codes, scales)
 
         def mx(out, codes, scales, a, n0, n1):

@@ -35,7 +35,7 @@ def tile_windowattentionblock_pa_t_kernel(tc, x, wq, bq, wk, bk, wv, bv, out_0, 
         if MANUAL:
             ctx.enter_context(tc.manual_schedule())
 
-        b_row = const.tile([P, 512], BF16, name="b_row")
+        b_row = const.tile([P, 384], BF16, name="b_row")
         nc.vector.memset(b_row[:], 0.0)
         ones = const.tile([P, P], BF16, name="ones")
         nc.vector.memset(ones[:], 1.0)
@@ -53,19 +53,23 @@ def tile_windowattentionblock_pa_t_kernel(tc, x, wq, bq, wk, bk, wv, bv, out_0, 
 
         x0 = xpool.tile([P, 4096], BF16, name="x0")
         x_sb[0] = x0[:]
+        def load_biases(ms):
+            for m in ms:
+                nc.sync.dma_start(
+                    out=b_row[0:1, m * P:(m + 1) * P],
+                    in_=biases[m].rearrange("(o h) d -> o (h d)", o=1),
+                )
+
         nc.sync.dma_start(out=x0[:, 2048:4096], in_=xc[32:32 + P, 2048:4096])
-        nc.sync.dma_start(out=x0[:, 0:2048], in_=xc[32:32 + P, 0:2048])
         for m in range(3):
             nc.sync.dma_start(
                 out=w_raw[:, m, :, :].rearrange("p (u e) f -> p u (e f)", u=2),
                 in_=weights[m].rearrange("(p u e) h d -> p u (e h d)", u=2, e=2),
             )
+        nc.sync.dma_start(out=x0[:, 0:2048], in_=xc[32:32 + P, 0:2048])
+        load_biases((0, 1))
         load_slabs(1, 1)
-        for m in range(3):
-            nc.sync.dma_start(
-                out=b_row[0:1, m * P:(m + 1) * P],
-                in_=biases[m].rearrange("(o h) d -> o (h d)", o=1),
-            )
+        load_biases((2,))
         load_slabs(2, 1)
         load_slabs(4, 1)
         xwrap = xpool.tile([P, 2, 4096], BF16, name="xwrap")
@@ -119,10 +123,10 @@ def tile_windowattentionblock_pa_t_kernel(tc, x, wq, bq, wk, bk, wv, bv, out_0, 
 
         bias_sb = const.tile([P, 3, P], F32, name="bias_sb")
 
-        def spread_bias():
+        def spread_bias(c0, c1):
             bias_ps = psum_o.tile([P, 512], F32, name="acc")
-            nc.tensor.matmul(out=bias_ps[:], lhsT=ones[:], rhs=b_row[:], start=True, stop=True)
-            nc.scalar.copy(out=bias_sb[:].rearrange("p m f -> p (m f)"), in_=bias_ps[:, 0:384])
+            nc.tensor.matmul(out=bias_ps[:, c0:c1], lhsT=ones[:], rhs=b_row[:, c0:c1], start=True, stop=True)
+            nc.scalar.copy(out=bias_sb[:].rearrange("p m f -> p (m f)")[:, c0:c1], in_=bias_ps[:, c0:c1])
 
         units = [(k, hb) for k in SLABS for hb in range(2)]
         state = {}
@@ -200,13 +204,12 @@ def tile_windowattentionblock_pa_t_kernel(tc, x, wq, bq, wk, bk, wv, bv, out_0, 
             )
             if half == 1:
                 v_sb = o_sb[:, 2, 4 * hb:4 * hb + 4, :]
-                nc.scalar.copy(out=v_sb, in_=zb[:])
-                nc.gpsimd.tensor_tensor(
-                    out=v_sb,
-                    in0=v_sb,
-                    in1=bias_sb[:, 2:3, :].to_broadcast([P, 4, P]),
-                    op=mybir.AluOpType.add,
-                )
+                bias_v = bias_sb[:, 2:3, :].to_broadcast([P, 4, P])
+                if h % 4 == 3:
+                    nc.vector.tensor_tensor(out=v_sb, in0=zb[:], in1=bias_v, op=mybir.AluOpType.add)
+                else:
+                    nc.scalar.copy(out=v_sb, in_=zb[:])
+                    nc.gpsimd.tensor_tensor(out=v_sb, in0=v_sb, in1=bias_v, op=mybir.AluOpType.add)
 
         def store(ti, t0, t1):
             o_sb = state[("o", ti)]
@@ -234,10 +237,12 @@ def tile_windowattentionblock_pa_t_kernel(tc, x, wq, bq, wk, bk, wv, bv, out_0, 
         for h in range(n_units):
             ti, hb = units[h]
             transposes_upto(h + min(LOOK_T, h + 1))
+            if h == 0:
+                spread_bias(0, 256)
             passes(h, 0)
             passes(h, 1)
             if h == 0:
-                spread_bias()
+                spread_bias(256, 384)
             quantise_upto(h + min(LOOK_Q, h + 1))
             finish(h, 0)
             finish(h, 1)

from contextlib import ExitStack

import concourse.mybir as mybir
from concourse.masks import make_identity

FP8X4 = mybir.dt.float8_e4m3fn_x4
BF16 = mybir.dt.bfloat16
F32 = mybir.dt.float32
U32 = mybir.dt.uint32
U8 = mybir.dt.uint8

P = 128
FLOPS = 2 * 8192 * 512 * 384
MANUAL = True
LOOK_T = 1
LOOK_Q = 1
SLABS = (0, 1, 2, 4, 3, 7, 5, 6)


def tile_windowattentionblock_pa_t_kernel(tc, x, wq, bq, wk, bk, wv, bv, out_0, out_1, out_2):
    nc = tc.nc
    weights = (wq, wk, wv)
    biases = (bq, bk, bv)
    outs = [o.rearrange("n (ti tj) h d -> (n ti) (tj h d)", tj=8) for o in (out_0, out_1, out_2)]
    xc = x.rearrange("b i (aj rj) c -> (b i aj) (rj c)", rj=8)

    with ExitStack() as ctx:
        const = ctx.enter_context(tc.tile_pool(name="const", bufs=1))
        xpool = ctx.enter_context(tc.tile_pool(name="xpool", bufs=1))
        gpool = ctx.enter_context(tc.tile_pool(name="gpool", bufs=3))
        qpool = ctx.enter_context(tc.tile_pool(name="qpool", bufs=4))
        opool = ctx.enter_context(tc.tile_pool(name="opool", bufs=8))
        psum_t = ctx.enter_context(tc.psum_pool(name="psum_t", bufs=2))
        psum_o = ctx.enter_context(tc.psum_pool(name="psum_o", bufs=6))
        if MANUAL:
            ctx.enter_context(tc.manual_schedule())

        b_row = const.tile([P, 384], BF16, name="b_row")
        nc.vector.memset(b_row[:], 0.0)
        ones = const.tile([P, P], BF16, name="ones")
        nc.vector.memset(ones[:], 1.0)

        w_raw = const.tile([P, 3, 4, P], BF16, name="w_raw")
        x_sb = {}

        def load_slabs(first, n):
            x_t = xpool.tile([P, n, 4096], BF16, name="x%d" % first)
            b, a = divmod(first, 4)
            c0 = (b * 64 + 16 * a + 4) * 8
            nc.sync.dma_start(out=x_t[:], in_=xc[c0:c0 + n * P, :].rearrange("(s p) f -> p s f", p=P))
            for i in range(n):
                x_sb[first + i] = x_t[:, i, :]

        x0 = xpool.tile([P, 4096], BF16, name="x0")
        x_sb[0] = x0[:]
        def load_biases(ms):
            for m in ms:
                nc.sync.dma_start(
                    out=b_row[0:1, m * P:(m + 1) * P],
                    in_=biases[m].rearrange("(o h) d -> o (h d)", o=1),
                )

        nc.sync.dma_start(out=x0[:, 2048:4096], in_=xc[32:32 + P, 2048:4096])
        for m in range(3):
            nc.sync.dma_start(
                out=w_raw[:, m, :, :].rearrange("p (u e) f -> p u (e f)", u=2),
                in_=weights[m].rearrange("(p u e) h d -> p u (e h d)", u=2, e=2),
            )
        nc.sync.dma_start(out=x0[:, 0:2048], in_=xc[32:32 + P, 0:2048])
        load_biases((0, 1))
        load_slabs(1, 1)
        load_biases((2,))
        load_slabs(2, 1)
        load_slabs(4, 1)
        xwrap = xpool.tile([P, 2, 4096], BF16, name="xwrap")
        xcb = xc.rearrange("(b c) f -> c b f", b=2)
        nc.sync.dma_start(out=xwrap[0:P:2, :, :], in_=xcb[416:480, :, :])
        nc.sync.dma_start(out=xwrap[1:P:4, :, :], in_=xcb[480:512, :, :])
        nc.sync.dma_start(out=xwrap[3:P:4, :, :], in_=xcb[0:32, :, :])
        x_sb[3] = xwrap[:, 0, :]
        x_sb[7] = xwrap[:, 1, :]
        load_slabs(5, 2)


        ident = const.tile([P, P], F32, name="ident")
        make_identity(nc, ident[:])
        pa = const.tile([P, P], F32, name="pa")
        pb = const.tile([P, P], F32, name="pb")
        src = ident[:].rearrange("p (g t a) -> p g a t", g=2, t=8)
        pav = pa[:].rearrange("p (g a t) -> p g a t", g=2, a=8)
        pbv = pb[:].rearrange("p (g a t) -> p g a t", g=2, a=8)
        nc.gpsimd.tensor_copy(out=pav, in_=src)
        nc.gpsimd.tensor_copy(out=pbv[:, :, 0:7, :], in_=src[:, :, 1:8, :])
        nc.gpsimd.tensor_copy(out=pbv[:, :, 7:8, :], in_=src[:, :, 0:1, :])
        paw = const.tile([P, P], F32, name="paw")
        pbw = const.tile([P, P], F32, name="pbw")
        src0 = ident[:, 0:P:2].rearrange("p (t a) -> p a t", t=8)
        src1 = ident[:].rearrange("p (tl a r) -> p r a tl", tl=4, a=8)
        for dst, shift in ((paw, 0), (pbw, 1)):
            d0 = dst[:, 0:64].rearrange("p (a t) -> p a t", a=8)
            d1 = dst[:, 64:P].rearrange("p (a th tl) -> p th a tl", a=8, th=2)
            nc.vector.tensor_copy(out=d0[:, 0:8 - shift, :], in_=src0[:, shift:8, :])
            nc.vector.tensor_copy(out=d1[:, :, 0:8 - shift, :], in_=src1[:, 1:4:2, shift:8, :])
            if shift:
                nc.vector.tensor_copy(out=d0[:, 7:8, :], in_=src0[:, 0:1, :])
                nc.vector.tensor_copy(out=d1[:, :, 7:8, :], in_=src1[:, 1:4:2, 0:1, :])

        w_grp = const.tile([P, 3, P, 4], BF16, name="w_grp", align_bytes=64)
        w_codes = const.tile([P, 384], U32, name="w_codes", align_bytes=64)
        w_scales = const.tile([P, 384], U8, name="w_scales", align_bytes=64)
        for m in range(3):
            nc.vector.tensor_copy(out=w_grp[:, m, :, :], in_=w_raw[:, m, :, :].rearrange("p t f -> p f t"))
        nc.vector.quantize_mx(
            out=w_codes[:, 0:256].bitcast(FP8X4),
            scales=w_scales[:, 0:256],
            in_=w_grp[:, 0:2, :, :].rearrange("p m f t -> p (m f t)"),
        )
        nc.vector.quantize_mx(
            out=w_codes[:, 256:384].bitcast(FP8X4),
            scales=w_scales[:, 256:384],
            in_=w_grp[:, 2, :, :].rearrange("p f t -> p (f t)"),
        )

        bias_sb = const.tile([P, 3, P], F32, name="bias_sb")

        def spread_bias(c0, c1):
            bias_ps = psum_o.tile([P, 512], F32, name="acc")
            nc.tensor.matmul(out=bias_ps[:, c0:c1], lhsT=ones[:], rhs=b_row[:, c0:c1], start=True, stop=True)
            nc.scalar.copy(out=bias_sb[:].rearrange("p m f -> p (m f)")[:, c0:c1], in_=bias_ps[:, c0:c1])

        units = [(k, hb) for k in SLABS for hb in range(2)]
        state = {}

        def transposes(h):
            ti, hb = units[h]
            if ti % 4 == 3:
                perm = paw if hb == 0 else pbw
            else:
                perm = pa if hb == 0 else pb
            xf = x_sb[ti].bitcast(F32)
            g = gpool.tile([P, 2048], BF16, name="g", align_bytes=64)
            gf = g[:].bitcast(F32).rearrange("p (a r u) -> p a r u", a=4, u=2)
            for a2 in range(2):
                xt = psum_t.tile([P, 2, 2, P], F32, name="xt")
                for a in range(2):
                    rj = (4 * hb + 2 * a2 + a + 4) % 8
                    for u in range(2):
                        c0 = rj * 256
                        nc.tensor.transpose(xt[:, a, u, :], xf[:, c0 + u:c0 + 256:2], perm[:])
                nc.scalar.copy(out=gf[:, 2 * a2:2 * a2 + 2, :, :], in_=xt[:].rearrange("p a u r -> p a r u"))
            state[("g", h)] = g

        def quantise(h):
            g = state[("g", h)]
            codes = qpool.tile([P, 512], U32, name="codes", align_bytes=64)
            scales = qpool.tile([P, 512], U8, name="scales", align_bytes=64)
            for half in range(2):
                cols = slice(half * 256, half * 256 + 256)
                nc.vector.quantize_mx(
                    out=codes[:, cols].bitcast(FP8X4),
                    scales=scales[:, cols],
                    in_=g[:, half * 1024:half * 1024 + 1024],
                )
            state[("q", h)] = (codes, scales)

        def mx(out, codes, scales, a, n0, n1):
            cols = slice(a * P, (a + 1) * P)
            nc.tensor.matmul_mx(
                out=out,
                lhsT=codes[:, cols].bitcast(FP8X4),
                lhsT_scale=scales[:, cols],
                rhs=w_codes[:, n0:n1].bitcast(FP8X4),
                rhs_scale=w_scales[:, n0:n1],
                start=True,
                stop=True,
            )

        def passes(h, half):
            ti, hb = units[h]
            codes, scales = state[("q", h)]
            if half == 0:
                state[("z", h)] = psum_o.tile([P, 4, P], F32, name="acc")
            zb = state[("z", h)]
            qk = psum_o.tile([P, 2, 2, P], F32, name="acc")
            for i in range(2):
                a = 2 * half + i
                mx(qk[:, i, :, :].rearrange("p m f -> p (m f)"), codes, scales, a, 0, 256)
                mx(zb[:, a, :], codes, scales, a, 256, 384)
            state[("qk", h, half)] = qk

        def finish(h, half):
            ti, hb = units[h]
            if hb == 0 and half == 0:
                state[("o", ti)] = opool.tile([P, 3, 8, P], F32, name="o_sb")
            o_sb = state[("o", ti)]
            zb = state[("z", h)]
            qk = state[("qk", h, half)]
            t0 = 4 * hb + 2 * half
            nc.vector.tensor_tensor(
                out=o_sb[:, 0:2, t0:t0 + 2, :],
                in0=qk[:].rearrange("p t m f -> p m t f"),
                in1=bias_sb[:, 0:2, :].unsqueeze(2).to_broadcast([P, 2, 2, P]),
                op=mybir.AluOpType.add,
            )
            if half == 1:
                v_sb = o_sb[:, 2, 4 * hb:4 * hb + 4, :]
                bias_v = bias_sb[:, 2:3, :].to_broadcast([P, 4, P])
                if h % 4 == 3:
                    nc.vector.tensor_tensor(out=v_sb, in0=zb[:], in1=bias_v, op=mybir.AluOpType.add)
                else:
                    nc.scalar.copy(out=v_sb, in_=zb[:])
                    nc.gpsimd.tensor_tensor(out=v_sb, in0=v_sb, in1=bias_v, op=mybir.AluOpType.add)

        def store(ti, t0, t1):
            o_sb = state[("o", ti)]
            for m in range(3):
                nc.sync.dma_start(
                    out=outs[m][ti * P:(ti + 1) * P, t0 * P:t1 * P],
                    in_=o_sb[:, m, t0:t1, :].rearrange("p t f -> p (t f)"),
                )

        n_units = len(units)
        done = {"t": 0, "q": 0}

        def transposes_upto(last):
            while done["t"] <= min(last, n_units - 1):
                transposes(done["t"])
                done["t"] += 1

        def quantise_upto(last):
            while done["q"] <= min(last, n_units - 1):
                quantise(done["q"])
                done["q"] += 1

        transposes_upto(0)
        quantise_upto(0)
        for h in range(n_units):
            ti, hb = units[h]
            transposes_upto(h + min(LOOK_T, h + 1))
            if h == 0:
                spread_bias(0, 256)
            passes(h, 0)
            passes(h, 1)
            if h == 0:
                spread_bias(256, 384)
            quantise_upto(h + min(LOOK_Q, h + 1))
            finish(h, 0)
            finish(h, 1)
            if h >= n_units - 6:
                store(ti, 4 * hb, 4 * hb + 4)
            elif hb == 1:
                store(ti, 0, 8)
